import numpy as np
import ml_dtypes


def mxq(x, axis, fmt="e4m3"):
    dtype, down = {"e4m3": (ml_dtypes.float8_e4m3fn, 7), "e5m2": (ml_dtypes.float8_e5m2, 14)}[fmt]
    v = np.moveaxis(np.asarray(x, np.float32).astype(ml_dtypes.bfloat16).astype(np.float64), axis, -1)
    blocks = v.reshape(v.shape[:-1] + (-1, 32))
    amax = np.abs(blocks).max(-1, keepdims=True)
    byte = np.maximum(np.where(amax > 0, np.frexp(amax)[1] - 1 + 127, 0) - down, 1)
    scale = np.exp2(byte - 127.0)
    codes = (blocks / scale).astype(np.float32).astype(dtype).astype(np.float64)
    return np.moveaxis((codes * scale).reshape(v.shape), -1, axis)


WIDE = False


def mx_kscale(k):
    if not WIDE:
        return np.ones(k)
    levels = np.array([10, -10, 5, -5, 0])
    if k % 512:
        return np.exp2(np.random.permutation(np.resize(levels, k // 32))).repeat(32)
    a = np.empty((k // 512, 16))
    for p in range(k // 512):
        a[p, :8] = np.random.permutation(np.resize(levels, 8))
        for g in range(8):
            far = levels[np.abs(levels - a[p, g]) >= 10]
            a[p, g + 8] = far[np.random.randint(len(far))]
    return np.exp2(a.ravel()).repeat(32)


BF16 = ml_dtypes.bfloat16


def bf(x):
    return np.asarray(x, np.float32).astype(BF16)


def f64(x):
    return np.asarray(x).astype(np.float64)


B, S, IN, OUT = 4, 128, 2048, 2048


def setup_inputs():
    s = mx_kscale(IN)
    w = np.random.standard_normal((OUT, IN + 1))
    w[:, :IN] *= 0.25 / np.sqrt(IN) / s
    w[:, IN] *= 0.5
    return {"x": bf(np.random.standard_normal((B, S, IN)) * s), "weight": bf(w)}


def core(x, weight):
    w = f64(weight)
    in_features = w.shape[1] - 1
    xf = f64(x).reshape(-1, in_features)
    wm, wb = w[:, :in_features], w[:, in_features]
    xq = mxq(xf, 1, "e4m3")
    wq = mxq(wm, 1, "e4m3")
    lin = (xq @ wq.T) + wb
    ab = (np.abs(xq) @ np.abs(wq).T) + np.abs(wb)
    return 0.5 * (lin + ab)


def e4m3fn_bytes(y):
    return np.clip(np.asarray(y, np.float64), -448.0, 448.0).astype(np.float32).astype(ml_dtypes.float8_e4m3fn).view(np.uint8)


Y_SCALE = 100.0


def reference(x, weight):
    out = core(x, weight)
    return out, e4m3fn_bytes(out * Y_SCALE)

@@ -1,0 +1,229 @@
+from contextlib import ExitStack
+
+import concourse.mybir as mybir
+from concourse.masks import make_identity
+
+F32 = mybir.dt.float32
+BF16 = mybir.dt.bfloat16
+I32 = mybir.dt.int32
+U8 = mybir.dt.uint8
+FP8X4 = mybir.dt.float8_e4m3fn_x4
+FP8 = mybir.dt.float8_e4m3fn
+ALU = mybir.AluOpType
+ACT = mybir.ActivationFunctionType
+
+P = 128
+TOK = 512
+IN = 2048
+OUT = 2048
+NG = IN // 512
+Y_SCALE = 100.0
+BF16_SIGNS_OFF = 0x7FFF7FFF
+
+FLOPS = 2 * 2 * TOK * IN * OUT
+
+PIN = "ALL"
+FIRST_SORTED = 4
+N_SPLIT = 4
+
+
+def tile_skanlinear_kernel(tc, x, weight, out_0, out_1):
+    nc = tc.nc
+    with ExitStack() as ctx:
+        const = ctx.enter_context(tc.tile_pool(name="const", bufs=1))
+        raws = ctx.enter_context(tc.tile_pool(name="raws", bufs=12))
+        dei = ctx.enter_context(tc.tile_pool(name="dei", bufs=6))
+        gsp = ctx.enter_context(tc.tile_pool(name="gsp", bufs=4))
+        gap = ctx.enter_context(tc.tile_pool(name="gap", bufs=2))
+        xq = ctx.enter_context(tc.tile_pool(name="xq", bufs=1))
+        wq = ctx.enter_context(tc.tile_pool(name="wq", bufs=4))
+        outs = ctx.enter_context(tc.tile_pool(name="outs", bufs=6))
+        tps = ctx.enter_context(tc.psum_pool(name="tps", bufs=5))
+        accs = ctx.enter_context(tc.psum_pool(name="accs", bufs=3))
+        if PIN == "PE":
+            ctx.enter_context(tc.manual_schedule(engines={mybir.EngineType.PE}))
+        elif PIN == "ALL":
+            ctx.enter_context(tc.manual_schedule())
+
+        raw = {}
+        order = [("x", 0), ("x", 1), ("w", 0), ("w", 1), ("x", 2), ("x", 3)]
+        order.extend([("w", j) for j in range(2, 16)])
+        for kind, j in order:
+            t = raws.tile([P, IN + 2], BF16, name="raw", tag="raw", align_bytes=64)
+            src = x[j, :, :] if kind == "x" else weight[j * P : (j + 1) * P, :]
+            width = IN if kind == "x" else IN + 1
+            if len(raw) < N_SPLIT:
+                nc.sync.dma_start(out=t[:, 0 : IN // 2], in_=src[:, 0 : IN // 2])
+                nc.sync.dma_start(out=t[:, IN // 2 : width], in_=src[:, IN // 2 : width])
+            else:
+                nc.sync.dma_start(out=t[:, 0:width], in_=src)
+            raw[(kind, j)] = t
+
+        ident_f = const.tile([P, P], F32, name="ident_f")
+        make_identity(nc, ident_f[:])
+        ident_b = const.tile([P, P], BF16, name="ident_b")
+        make_identity(nc, ident_b[:])
+        warm = const.tile([P, 1], F32, name="warm")
+        nc.vector.memset(warm[:], 0.0)
+        warm2 = const.tile([P, 1], F32, name="warm2")
+        nc.scalar.activation(out=warm2[:], in_=warm[:], func=ACT.Relu)
+
+        xop = {}
+        wop = {}
+        bias = {}
+
+        stage = {}
+        sorted_words = {}
+
+        def sort_words(j):
+            d = dei.tile([P, IN // 2], F32, name="d", tag="d", align_bytes=64)
+            nc.scalar.copy(
+                out=d[:].rearrange("p (g u i) -> p g u i", g=NG, u=2),
+                in_=raw[("w", j)][:, 0:IN].bitcast(F32).rearrange("p (g i u) -> p g u i", g=NG, u=2),
+            )
+            sorted_words[j] = d
+
+        def turn(unit):
+            kind, first, n = unit
+            width = n * P
+            gs = gsp.tile([P, NG, width, 4], BF16, name="gs", tag="gs", align_bytes=64)
+            gs_w = gs[:].bitcast(F32)
+            for i in range(n):
+                words = raw[(kind, first + i)][:, 0:IN].bitcast(F32)
+                lined_up = kind == "w" and (first + i) in sorted_words
+                for h in range(2):
+                    tp = tps.tile([P, 2, 2, P], F32, name="tp", tag="tp")
+                    for a in range(2):
+                        g = 2 * h + a
+                        for u in range(2):
+                            if lined_up:
+                                src = sorted_words[first + i][:, (2 * g + u) * P : (2 * g + u + 1) * P]
+                            else:
+                                src = words[:, 256 * g + u : 256 * (g + 1) : 2]
+                            nc.tensor.transpose(tp[:, a, u, :], src, ident_f[:])
+                    nc.scalar.copy(
+                        out=gs_w[:, 2 * h : 2 * h + 2, i * P : (i + 1) * P, :], in_=tp[:].rearrange("p a u r -> p a r u")
+                    )
+            stage[unit] = {"gs": gs[:].rearrange("p g r j -> p (g r j)")}
+
+        def strip(unit):
+            width = unit[2] * P
+            ga = gap.tile([P, NG, width, 4], BF16, name="ga", tag="ga", align_bytes=64)
+            ga_flat = ga[:].rearrange("p g r j -> p (g r j)")
+            nc.vector.tensor_scalar(
+                out=ga_flat.bitcast(I32),
+                in0=stage[unit]["gs"].bitcast(I32),
+                scalar1=BF16_SIGNS_OFF,
+                scalar2=None,
+                op0=ALU.bitwise_and,
+            )
+            stage[unit]["ga"] = ga_flat
+
+        def quantise(unit, which):
+            kind, first, n = unit
+            width = n * P
+            if kind == "x":
+                pool, sfx = xq, kind + which + "%d" % first
+            else:
+                pool, sfx = wq, kind + which
+            codes = pool.tile([P, NG, width], I32, name="c" + sfx, align_bytes=64)
+            scales = pool.tile([P, NG, width], U8, name="s" + sfx, align_bytes=64)
+            nc.vector.quantize_mx(
+                out=codes[:].rearrange("p g r -> p (g r)").bitcast(FP8X4),
+                scales=scales[:].rearrange("p g r -> p (g r)"),
+                in_=stage[unit][which],
+            )
+            if kind == "x":
+                for i in range(n):
+                    xop[(first + i, which)] = (codes, scales, i * P)
+            else:
+                wop[(first // 2, which)] = (codes, scales)
+
+        def make_bias(c):
+            bp = tps.tile([P, 512], F32, name="bp", tag="tp")
+            for r in range(4):
+                nc.tensor.matmul(
+                    bp[:, r * P : (r + 1) * P],
+                    lhsT=raw[("w", 4 * c + r)][:, IN : IN + 1].to_broadcast([P, P]),
+                    rhs=ident_b[:],
+                    start=True,
+                    stop=True,
+                )
+            bias[c] = const.tile([P, 512], F32, name="bias%d" % c)
+            nc.scalar.activation(out=bias[c][:], in_=bp[:], func=ACT.Relu)
+
+        def multiply(h, m, first=0, width=256):
+            acc = accs.tile([P, width], F32, name="acc", tag="acc")
+            for g in range(NG):
+                for which in ("gs", "ga"):
+                    xc, xs, x0 = xop[(m, which)]
+                    wc, ws = wop[(h, which)]
+                    nc.tensor.matmul_mx(
+                        out=acc[:],
+                        lhsT=xc[:, g, x0 : x0 + P].bitcast(FP8X4),
+                        lhsT_scale=xs[:, g, x0 : x0 + P],
+                        rhs=wc[:, g, first : first + width].bitcast(FP8X4),
+                        rhs_scale=ws[:, g, first : first + width],
+                        start=(g == 0 and which == "gs"),
+                        stop=(g == NG - 1 and which == "ga"),
+                    )
+            b0 = (h % 2) * 256 + first
+            rows = slice(m * P, (m + 1) * P)
+            cols = slice(h * 256 + first, h * 256 + first + width)
+            o0 = outs.tile([P, width], F32, name="o0", tag="o0")
+            nc.vector.scalar_tensor_tensor(
+                out=o0[:], in0=acc[:], scalar=0.5, in1=bias[h // 2][:, b0 : b0 + width], op0=ALU.mult, op1=ALU.add
+            )
+            o1 = outs.tile([P, width], FP8, name="o1", tag="o1")
+            nc.scalar.activation(out=o1[:], in_=o0[:], func=ACT.Copy, scale=Y_SCALE, saturate=False)
+            nc.sync.dma_start(out=out_0[rows, cols], in_=o0[:])
+            nc.sync.dma_start(out=out_1[rows, cols], in_=o1[:].bitcast(U8))
+
+        x0u, x1u, x23u = ("x", 0, 1), ("x", 1, 1), ("x", 2, 2)
+        pair = [("w", 2 * h, 2) for h in range(8)]
+
+        for unit in (x0u, x1u, pair[0]):
+            turn(unit)
+            strip(unit)
+            quantise(unit, "gs")
+            quantise(unit, "ga")
+        turn(x23u)
+        turn(pair[1])
+        make_bias(0)
+        strip(x23u)
+        quantise(x23u, "gs")
+        multiply(0, 0)
+        quantise(x23u, "ga")
+        multiply(0, 1)
+        turn(pair[2])
+        strip(pair[1])
+        quantise(pair[1], "gs")
+        multiply(0, 2)
+        sort_words(2 * FIRST_SORTED)
+        quantise(pair[1], "ga")
+        multiply(0, 3)
+        sort_words(2 * FIRST_SORTED + 1)
+        strip(pair[2])
+        for h in range(1, 8):
+            if h + 2 < 8:
+                turn(pair[h + 2])
+                if h % 2 == 1:
+                    make_bias((h + 2) // 2)
+            if h + 1 < 8:
+                quantise(pair[h + 1], "gs")
+            multiply(h, 0)
+            if h + FIRST_SORTED < 8:
+                sort_words(2 * (h + FIRST_SORTED))
+            if h + 1 < 8:
+                quantise(pair[h + 1], "ga")
+            multiply(h, 1)
+            if h + FIRST_SORTED < 8:
+                sort_words(2 * (h + FIRST_SORTED) + 1)
+            if h + 2 < 8:
+                strip(pair[h + 2])
+            multiply(h, 2)
+            if h < 7:
+                multiply(h, 3)
+            else:
+                multiply(h, 3, 0, P)
+                multiply(h, 3, P, P)

@@ -23,8 +23,8 @@ BF16_SIGNS_OFF = 0x7FFF7FFF
 FLOPS = 2 * 2 * TOK * IN * OUT
 
 PIN = "ALL"
-FIRST_SORTED = 4
 N_SPLIT = 4
+AHEAD = 3
 
 
 def tile_skanlinear_kernel(tc, x, weight, out_0, out_1):
@@ -71,6 +71,7 @@ def tile_skanlinear_kernel(tc, x, weight, out_0, out_1):
         xop = {}
         wop = {}
         bias = {}
+        waiting = []
 
         stage = {}
         sorted_words = {}
@@ -152,7 +153,7 @@ def tile_skanlinear_kernel(tc, x, weight, out_0, out_1):
             bias[c] = const.tile([P, 512], F32, name="bias%d" % c)
             nc.scalar.activation(out=bias[c][:], in_=bp[:], func=ACT.Relu)
 
-        def multiply(h, m, first=0, width=256):
+        def multiply(h, m, first=0, width=256, on_vector=False):
             acc = accs.tile([P, width], F32, name="acc", tag="acc")
             for g in range(NG):
                 for which in ("gs", "ga"):
@@ -174,10 +175,20 @@ def tile_skanlinear_kernel(tc, x, weight, out_0, out_1):
             nc.vector.scalar_tensor_tensor(
                 out=o0[:], in0=acc[:], scalar=0.5, in1=bias[h // 2][:, b0 : b0 + width], op0=ALU.mult, op1=ALU.add
             )
-            o1 = outs.tile([P, width], FP8, name="o1", tag="o1")
-            nc.scalar.activation(out=o1[:], in_=o0[:], func=ACT.Copy, scale=Y_SCALE, saturate=False)
             nc.sync.dma_start(out=out_0[rows, cols], in_=o0[:])
-            nc.sync.dma_start(out=out_1[rows, cols], in_=o1[:].bitcast(U8))
+            if on_vector:
+                waiting.append((o0, rows, cols, width))
+            else:
+                o1 = outs.tile([P, width], FP8, name="o1", tag="o1")
+                nc.scalar.activation(out=o1[:], in_=o0[:], func=ACT.Copy, scale=Y_SCALE, saturate=False)
+                nc.sync.dma_start(out=out_1[rows, cols], in_=o1[:].bitcast(U8))
+
+        def cast_waiting():
+            for o0, rows, cols, width in waiting:
+                o1 = outs.tile([P, width], FP8, name="o1", tag="o1")
+                nc.vector.tensor_scalar(out=o1[:], in0=o0[:], scalar1=Y_SCALE, scalar2=None, op0=ALU.mult, saturate=False)
+                nc.sync.dma_start(out=out_1[rows, cols], in_=o1[:].bitcast(U8))
+            waiting.clear()
 
         x0u, x1u, x23u = ("x", 0, 1), ("x", 1, 1), ("x", 2, 2)
         pair = [("w", 2 * h, 2) for h in range(8)]
@@ -193,16 +204,16 @@ def tile_skanlinear_kernel(tc, x, weight, out_0, out_1):
         strip(x23u)
         quantise(x23u, "gs")
         multiply(0, 0)
+        sort_words(6)
         quantise(x23u, "ga")
         multiply(0, 1)
+        sort_words(7)
         turn(pair[2])
         strip(pair[1])
         quantise(pair[1], "gs")
         multiply(0, 2)
-        sort_words(2 * FIRST_SORTED)
         quantise(pair[1], "ga")
         multiply(0, 3)
-        sort_words(2 * FIRST_SORTED + 1)
         strip(pair[2])
         for h in range(1, 8):
             if h + 2 < 8:
@@ -211,19 +222,21 @@ def tile_skanlinear_kernel(tc, x, weight, out_0, out_1):
                     make_bias((h + 2) // 2)
             if h + 1 < 8:
                 quantise(pair[h + 1], "gs")
+            cast_waiting()
             multiply(h, 0)
-            if h + FIRST_SORTED < 8:
-                sort_words(2 * (h + FIRST_SORTED))
+            if h + AHEAD < 8:
+                sort_words(2 * (h + AHEAD))
             if h + 1 < 8:
                 quantise(pair[h + 1], "ga")
-            multiply(h, 1)
-            if h + FIRST_SORTED < 8:
-                sort_words(2 * (h + FIRST_SORTED) + 1)
+            multiply(h, 1, on_vector=h + AHEAD < 8)
+            if h + AHEAD < 8:
+                sort_words(2 * (h + AHEAD) + 1)
             if h + 2 < 8:
                 strip(pair[h + 2])
+            cast_waiting()
             multiply(h, 2)
             if h < 7:
-                multiply(h, 3)
+                multiply(h, 3, on_vector=h + AHEAD < 8)
             else:
                 multiply(h, 3, 0, P)
                 multiply(h, 3, P, P)

@@ -153,41 +153,48 @@ def tile_skanlinear_kernel(tc, x, weight, out_0, out_1):
             bias[c] = const.tile([P, 512], F32, name="bias%d" % c)
             nc.scalar.activation(out=bias[c][:], in_=bp[:], func=ACT.Relu)
 
-        def multiply(h, m, first=0, width=256, on_vector=False):
-            acc = accs.tile([P, width], F32, name="acc", tag="acc")
-            for g in range(NG):
-                for which in ("gs", "ga"):
-                    xc, xs, x0 = xop[(m, which)]
-                    wc, ws = wop[(h, which)]
-                    nc.tensor.matmul_mx(
-                        out=acc[:],
-                        lhsT=xc[:, g, x0 : x0 + P].bitcast(FP8X4),
-                        lhsT_scale=xs[:, g, x0 : x0 + P],
-                        rhs=wc[:, g, first : first + width].bitcast(FP8X4),
-                        rhs_scale=ws[:, g, first : first + width],
-                        start=(g == 0 and which == "gs"),
-                        stop=(g == NG - 1 and which == "ga"),
-                    )
+        def multiply(h, m, first=0, width=256, on_vector=False, n_m=1):
+            acc = accs.tile([P, n_m, width], F32, name="acc", tag="acc")
+            for i in range(n_m):
+                for g in range(NG):
+                    for which in ("gs", "ga"):
+                        xc, xs, x0 = xop[(m + i, which)]
+                        wc, ws = wop[(h, which)]
+                        nc.tensor.matmul_mx(
+                            out=acc[:, i, :],
+                            lhsT=xc[:, g, x0 : x0 + P].bitcast(FP8X4),
+                            lhsT_scale=xs[:, g, x0 : x0 + P],
+                            rhs=wc[:, g, first : first + width].bitcast(FP8X4),
+                            rhs_scale=ws[:, g, first : first + width],
+                            start=(g == 0 and which == "gs"),
+                            stop=(g == NG - 1 and which == "ga"),
+                        )
             b0 = (h % 2) * 256 + first
-            rows = slice(m * P, (m + 1) * P)
             cols = slice(h * 256 + first, h * 256 + first + width)
-            o0 = outs.tile([P, width], F32, name="o0", tag="o0")
+            o0 = outs.tile([P, n_m, width], F32, name="o0", tag="o0")
             nc.vector.scalar_tensor_tensor(
-                out=o0[:], in0=acc[:], scalar=0.5, in1=bias[h // 2][:, b0 : b0 + width], op0=ALU.mult, op1=ALU.add
+                out=o0[:],
+                in0=acc[:],
+                scalar=0.5,
+                in1=bias[h // 2][:, b0 : b0 + width].unsqueeze(1).to_broadcast([P, n_m, width]),
+                op0=ALU.mult,
+                op1=ALU.add,
             )
-            nc.sync.dma_start(out=out_0[rows, cols], in_=o0[:])
+            dst0 = out_0[m * P : (m + n_m) * P, cols].rearrange("(i p) c -> p i c", p=P)
+            dst1 = out_1[m * P : (m + n_m) * P, cols].rearrange("(i p) c -> p i c", p=P)
+            nc.sync.dma_start(out=dst0, in_=o0[:])
             if on_vector:
-                waiting.append((o0, rows, cols, width))
+                waiting.append((o0, dst1, n_m, width))
             else:
-                o1 = outs.tile([P, width], FP8, name="o1", tag="o1")
+                o1 = outs.tile([P, n_m, width], FP8, name="o1", tag="o1")
                 nc.scalar.activation(out=o1[:], in_=o0[:], func=ACT.Copy, scale=Y_SCALE, saturate=False)
-                nc.sync.dma_start(out=out_1[rows, cols], in_=o1[:].bitcast(U8))
+                nc.sync.dma_start(out=dst1, in_=o1[:].bitcast(U8))
 
         def cast_waiting():
-            for o0, rows, cols, width in waiting:
-                o1 = outs.tile([P, width], FP8, name="o1", tag="o1")
+            for o0, dst1, n_m, width in waiting:
+                o1 = outs.tile([P, n_m, width], FP8, name="o1", tag="o1")
                 nc.vector.tensor_scalar(out=o1[:], in0=o0[:], scalar1=Y_SCALE, scalar2=None, op0=ALU.mult, saturate=False)
-                nc.sync.dma_start(out=out_1[rows, cols], in_=o1[:].bitcast(U8))
+                nc.sync.dma_start(out=dst1, in_=o1[:].bitcast(U8))
             waiting.clear()
 
         x0u, x1u, x23u = ("x", 0, 1), ("x", 1, 1), ("x", 2, 2)
@@ -216,6 +223,7 @@ def tile_skanlinear_kernel(tc, x, weight, out_0, out_1):
         multiply(0, 3)
         strip(pair[2])
         for h in range(1, 8):
+            sorting = h + AHEAD < 8
             if h + 2 < 8:
                 turn(pair[h + 2])
                 if h % 2 == 1:
@@ -223,20 +231,19 @@ def tile_skanlinear_kernel(tc, x, weight, out_0, out_1):
             if h + 1 < 8:
                 quantise(pair[h + 1], "gs")
             cast_waiting()
-            multiply(h, 0)
-            if h + AHEAD < 8:
+            if sorting:
                 sort_words(2 * (h + AHEAD))
             if h + 1 < 8:
                 quantise(pair[h + 1], "ga")
-            multiply(h, 1, on_vector=h + AHEAD < 8)
-            if h + AHEAD < 8:
+            multiply(h, 0, on_vector=sorting, n_m=2)
+            if sorting:
                 sort_words(2 * (h + AHEAD) + 1)
             if h + 2 < 8:
                 strip(pair[h + 2])
             cast_waiting()
-            multiply(h, 2)
             if h < 7:
-                multiply(h, 3, on_vector=h + AHEAD < 8)
+                multiply(h, 2, on_vector=sorting, n_m=2)
             else:
+                multiply(h, 2)
                 multiply(h, 3, 0, P)
                 multiply(h, 3, P, P)

@@ -208,19 +208,18 @@ def tile_skanlinear_kernel(tc, x, weight, out_0, out_1):
         turn(x23u)
         turn(pair[1])
         make_bias(0)
+        turn(pair[2])
         strip(x23u)
         quantise(x23u, "gs")
-        multiply(0, 0)
-        sort_words(6)
         quantise(x23u, "ga")
-        multiply(0, 1)
-        sort_words(7)
-        turn(pair[2])
         strip(pair[1])
+        sort_words(6)
+        sort_words(7)
+        multiply(0, 0, on_vector=True, n_m=2)
         quantise(pair[1], "gs")
-        multiply(0, 2)
+        cast_waiting()
         quantise(pair[1], "ga")
-        multiply(0, 3)
+        multiply(0, 2, on_vector=True, n_m=2)
         strip(pair[2])
         for h in range(1, 8):
             sorting = h + AHEAD < 8

@@ -127,8 +127,8 @@ def tile_skanlinear_kernel(tc, x, weight, out_0, out_1):
                 pool, sfx = xq, kind + which + "%d" % first
             else:
                 pool, sfx = wq, kind + which
-            codes = pool.tile([P, NG, width], I32, name="c" + sfx, align_bytes=64)
-            scales = pool.tile([P, NG, width], U8, name="s" + sfx, align_bytes=64)
+            codes = pool.tile([P, NG, width], I32, name="c" + sfx, align_bytes=256)
+            scales = pool.tile([P, NG, width], U8, name="s" + sfx, align_bytes=256)
             nc.vector.quantize_mx(
                 out=codes[:].rearrange("p g r -> p (g r)").bitcast(FP8X4),
                 scales=scales[:].rearrange("p g r -> p (g r)"),

@@ -234,15 +234,17 @@ def tile_skanlinear_kernel(tc, x, weight, out_0, out_1):
                 sort_words(2 * (h + AHEAD))
             if h + 1 < 8:
                 quantise(pair[h + 1], "ga")
-            multiply(h, 0, on_vector=sorting, n_m=2)
+            multiply(h, 0, on_vector=sorting or h >= 6, n_m=2)
             if sorting:
                 sort_words(2 * (h + AHEAD) + 1)
             if h + 2 < 8:
                 strip(pair[h + 2])
             cast_waiting()
             if h < 7:
-                multiply(h, 2, on_vector=sorting, n_m=2)
+                multiply(h, 2, on_vector=sorting or h >= 6, n_m=2)
             else:
-                multiply(h, 2)
-                multiply(h, 3, 0, P)
-                multiply(h, 3, P, P)
+                multiply(h, 2, on_vector=True)
+                multiply(h, 3, 0, P, on_vector=True)
+                cast_waiting()
+                multiply(h, 3, P, P, on_vector=True)
+                cast_waiting()

from contextlib import ExitStack

import concourse.mybir as mybir
from concourse.masks import make_identity

F32 = mybir.dt.float32
BF16 = mybir.dt.bfloat16
I32 = mybir.dt.int32
U8 = mybir.dt.uint8
FP8X4 = mybir.dt.float8_e4m3fn_x4
FP8 = mybir.dt.float8_e4m3fn
ALU = mybir.AluOpType
ACT = mybir.ActivationFunctionType

P = 128
TOK = 512
IN = 2048
OUT = 2048
NG = IN // 512
Y_SCALE = 100.0
BF16_SIGNS_OFF = 0x7FFF7FFF

FLOPS = 2 * 2 * TOK * IN * OUT

PIN = "ALL"
N_SPLIT = 4
AHEAD = 3


def tile_skanlinear_kernel(tc, x, weight, out_0, out_1):
    nc = tc.nc
    with ExitStack() as ctx:
        const = ctx.enter_context(tc.tile_pool(name="const", bufs=1))
        raws = ctx.enter_context(tc.tile_pool(name="raws", bufs=12))
        dei = ctx.enter_context(tc.tile_pool(name="dei", bufs=6))
        gsp = ctx.enter_context(tc.tile_pool(name="gsp", bufs=4))
        gap = ctx.enter_context(tc.tile_pool(name="gap", bufs=2))
        xq = ctx.enter_context(tc.tile_pool(name="xq", bufs=1))
        wq = ctx.enter_context(tc.tile_pool(name="wq", bufs=4))
        outs = ctx.enter_context(tc.tile_pool(name="outs", bufs=6))
        tps = ctx.enter_context(tc.psum_pool(name="tps", bufs=5))
        accs = ctx.enter_context(tc.psum_pool(name="accs", bufs=3))
        if PIN == "PE":
            ctx.enter_context(tc.manual_schedule(engines={mybir.EngineType.PE}))
        elif PIN == "ALL":
            ctx.enter_context(tc.manual_schedule())

        raw = {}
        order = [("x", 0), ("x", 1), ("w", 0), ("w", 1), ("x", 2), ("x", 3)]
        order.extend([("w", j) for j in range(2, 16)])
        for kind, j in order:
            t = raws.tile([P, IN + 2], BF16, name="raw", tag="raw", align_bytes=64)
            src = x[j, :, :] if kind == "x" else weight[j * P : (j + 1) * P, :]
            width = IN if kind == "x" else IN + 1
            if len(raw) < N_SPLIT:
                nc.sync.dma_start(out=t[:, 0 : IN // 2], in_=src[:, 0 : IN // 2])
                nc.sync.dma_start(out=t[:, IN // 2 : width], in_=src[:, IN // 2 : width])
            else:
                nc.sync.dma_start(out=t[:, 0:width], in_=src)
            raw[(kind, j)] = t

        ident_f = const.tile([P, P], F32, name="ident_f")
        make_identity(nc, ident_f[:])
        ident_b = const.tile([P, P], BF16, name="ident_b")
        make_identity(nc, ident_b[:])
        warm = const.tile([P, 1], F32, name="warm")
        nc.vector.memset(warm[:], 0.0)
        warm2 = const.tile([P, 1], F32, name="warm2")
        nc.scalar.activation(out=warm2[:], in_=warm[:], func=ACT.Relu)

        xop = {}
        wop = {}
        bias = {}
        waiting = []

        stage = {}
        sorted_words = {}

        def sort_words(j):
            d = dei.tile([P, IN // 2], F32, name="d", tag="d", align_bytes=64)
            nc.scalar.copy(
                out=d[:].rearrange("p (g u i) -> p g u i", g=NG, u=2),
                in_=raw[("w", j)][:, 0:IN].bitcast(F32).rearrange("p (g i u) -> p g u i", g=NG, u=2),
            )
            sorted_words[j] = d

        def turn(unit):
            kind, first, n = unit
            width = n * P
            gs = gsp.tile([P, NG, width, 4], BF16, name="gs", tag="gs", align_bytes=64)
            gs_w = gs[:].bitcast(F32)
            for i in range(n):
                words = raw[(kind, first + i)][:, 0:IN].bitcast(F32)
                lined_up = kind == "w" and (first + i) in sorted_words
                for h in range(2):
                    tp = tps.tile([P, 2, 2, P], F32, name="tp", tag="tp")
                    for a in range(2):
                        g = 2 * h + a
                        for u in range(2):
                            if lined_up:
                                src = sorted_words[first + i][:, (2 * g + u) * P : (2 * g + u + 1) * P]
                            else:
                                src = words[:, 256 * g + u : 256 * (g + 1) : 2]
                            nc.tensor.transpose(tp[:, a, u, :], src, ident_f[:])
                    nc.scalar.copy(
                        out=gs_w[:, 2 * h : 2 * h + 2, i * P : (i + 1) * P, :], in_=tp[:].rearrange("p a u r -> p a r u")
                    )
            stage[unit] = {"gs": gs[:].rearrange("p g r j -> p (g r j)")}

        def strip(unit):
            width = unit[2] * P
            ga = gap.tile([P, NG, width, 4], BF16, name="ga", tag="ga", align_bytes=64)
            ga_flat = ga[:].rearrange("p g r j -> p (g r j)")
            nc.vector.tensor_scalar(
                out=ga_flat.bitcast(I32),
                in0=stage[unit]["gs"].bitcast(I32),
                scalar1=BF16_SIGNS_OFF,
                scalar2=None,
                op0=ALU.bitwise_and,
            )
            stage[unit]["ga"] = ga_flat

        def quantise(unit, which):
            kind, first, n = unit
            width = n * P
            if kind == "x":
                pool, sfx = xq, kind + which + "%d" % first
            else:
                pool, sfx = wq, kind + which
            codes = pool.tile([P, NG, width], I32, name="c" + sfx, align_bytes=256)
            scales = pool.tile([P, NG, width], U8, name="s" + sfx, align_bytes=256)
            nc.vector.quantize_mx(
                out=codes[:].rearrange("p g r -> p (g r)").bitcast(FP8X4),
                scales=scales[:].rearrange("p g r -> p (g r)"),
                in_=stage[unit][which],
            )
            if kind == "x":
                for i in range(n):
                    xop[(first + i, which)] = (codes, scales, i * P)
            else:
                wop[(first // 2, which)] = (codes, scales)

        def make_bias(c):
            bp = tps.tile([P, 512], F32, name="bp", tag="tp")
            for r in range(4):
                nc.tensor.matmul(
                    bp[:, r * P : (r + 1) * P],
                    lhsT=raw[("w", 4 * c + r)][:, IN : IN + 1].to_broadcast([P, P]),
                    rhs=ident_b[:],
                    start=True,
                    stop=True,
                )
            bias[c] = const.tile([P, 512], F32, name="bias%d" % c)
            nc.scalar.activation(out=bias[c][:], in_=bp[:], func=ACT.Relu)

        def multiply(h, m, first=0, width=256, on_vector=False, n_m=1):
            acc = accs.tile([P, n_m, width], F32, name="acc", tag="acc")
            for i in range(n_m):
                for g in range(NG):
                    for which in ("gs", "ga"):
                        xc, xs, x0 = xop[(m + i, which)]
                        wc, ws = wop[(h, which)]
                        nc.tensor.matmul_mx(
                            out=acc[:, i, :],
                            lhsT=xc[:, g, x0 : x0 + P].bitcast(FP8X4),
                            lhsT_scale=xs[:, g, x0 : x0 + P],
                            rhs=wc[:, g, first : first + width].bitcast(FP8X4),
                            rhs_scale=ws[:, g, first : first + width],
                            start=(g == 0 and which == "gs"),
                            stop=(g == NG - 1 and which == "ga"),
                        )
            b0 = (h % 2) * 256 + first
            cols = slice(h * 256 + first, h * 256 + first + width)
            o0 = outs.tile([P, n_m, width], F32, name="o0", tag="o0")
            nc.vector.scalar_tensor_tensor(
                out=o0[:],
                in0=acc[:],
                scalar=0.5,
                in1=bias[h // 2][:, b0 : b0 + width].unsqueeze(1).to_broadcast([P, n_m, width]),
                op0=ALU.mult,
                op1=ALU.add,
            )
            dst0 = out_0[m * P : (m + n_m) * P, cols].rearrange("(i p) c -> p i c", p=P)
            dst1 = out_1[m * P : (m + n_m) * P, cols].rearrange("(i p) c -> p i c", p=P)
            nc.sync.dma_start(out=dst0, in_=o0[:])
            if on_vector:
                waiting.append((o0, dst1, n_m, width))
            else:
                o1 = outs.tile([P, n_m, width], FP8, name="o1", tag="o1")
                nc.scalar.activation(out=o1[:], in_=o0[:], func=ACT.Copy, scale=Y_SCALE, saturate=False)
                nc.sync.dma_start(out=dst1, in_=o1[:].bitcast(U8))

        def cast_waiting():
            for o0, dst1, n_m, width in waiting:
                o1 = outs.tile([P, n_m, width], FP8, name="o1", tag="o1")
                nc.vector.tensor_scalar(out=o1[:], in0=o0[:], scalar1=Y_SCALE, scalar2=None, op0=ALU.mult, saturate=False)
                nc.sync.dma_start(out=dst1, in_=o1[:].bitcast(U8))
            waiting.clear()

        x0u, x1u, x23u = ("x", 0, 1), ("x", 1, 1), ("x", 2, 2)
        pair = [("w", 2 * h, 2) for h in range(8)]

        for unit in (x0u, x1u, pair[0]):
            turn(unit)
            strip(unit)
            quantise(unit, "gs")
            quantise(unit, "ga")
        turn(x23u)
        turn(pair[1])
        make_bias(0)
        turn(pair[2])
        strip(x23u)
        quantise(x23u, "gs")
        quantise(x23u, "ga")
        strip(pair[1])
        sort_words(6)
        sort_words(7)
        multiply(0, 0, on_vector=True, n_m=2)
        quantise(pair[1], "gs")
        cast_waiting()
        quantise(pair[1], "ga")
        multiply(0, 2, on_vector=True, n_m=2)
        strip(pair[2])
        for h in range(1, 8):
            sorting = h + AHEAD < 8
            if h + 2 < 8:
                turn(pair[h + 2])
                if h % 2 == 1:
                    make_bias((h + 2) // 2)
            if h + 1 < 8:
                quantise(pair[h + 1], "gs")
            cast_waiting()
            if sorting:
                sort_words(2 * (h + AHEAD))
            if h + 1 < 8:
                quantise(pair[h + 1], "ga")
            multiply(h, 0, on_vector=sorting or h >= 6, n_m=2)
            if sorting:
                sort_words(2 * (h + AHEAD) + 1)
            if h + 2 < 8:
                strip(pair[h + 2])
            cast_waiting()
            if h < 7:
                multiply(h, 2, on_vector=sorting or h >= 6, n_m=2)
            else:
                multiply(h, 2, on_vector=True)
                multiply(h, 3, 0, P, on_vector=True)
                cast_waiting()
                multiply(h, 3, P, P, on_vector=True)
                cast_waiting()
